import numpy as np
import ml_dtypes

BF16 = ml_dtypes.bfloat16


def bf(x):
    return np.asarray(x, np.float32).astype(BF16)


def f32(x):
    return np.asarray(x, np.float32)


def f64(x):
    return np.asarray(x).astype(np.float64)


def striped(idx):
    return np.tile(idx.reshape(-1, 16).T, (8, 1))


D, S, N, M = 128, 256, 512, 128


def setup_inputs():
    r = 1.0 / np.sqrt(D)
    return {"x": f32(np.random.standard_normal((D, S))), "left": f32(np.random.standard_normal((D, N))), "wl": bf(np.random.uniform(-r, r, (D, D))), "bl": f32(0.1 * np.random.standard_normal((D, 1))), "wp": bf(np.random.uniform(-r, r, (D, M))), "bp": f32(0.1 * np.random.standard_normal((M, 1))), "offs": striped(np.random.permutation(np.tile(np.arange(S), 2))[:N])}


def reference(x, left, wl, bl, wp, bp, offs):
    idx = offs[:16].T.reshape(-1)
    s = f64(x)[:, idx] + f64(left)
    h = np.maximum(f64(wl).T @ s + 2.0 * f64(bl), 0.0)
    return f64(wp).T @ h + f64(bp)

@@ -1,0 +1,63 @@
+import concourse.mybir as mybir
+
+F32 = mybir.dt.float32
+BF16 = mybir.dt.bfloat16
+U16 = mybir.dt.uint16
+ADD = mybir.AluOpType.add
+RELU = mybir.ActivationFunctionType.Relu
+IDENTITY = mybir.ActivationFunctionType.Identity
+
+D, S, N, M = 128, 256, 512, 128
+PIECE = 256
+PIECE_OFFSET_COLUMNS = PIECE // 16
+
+FLOPS = 2 * D * D * N + 2 * D * M * N
+
+
+def tile_rnn_model_kernel(tc, x, left, wl, bl, wp, bp, offs, out):
+    nc = tc.nc
+    with (
+        tc.tile_pool(name="held", bufs=1) as held,
+        tc.tile_pool(name="work", bufs=2) as work,
+        tc.psum_pool(name="psum", bufs=2) as psum,
+    ):
+        offsets = held.tile([D, N // 16], U16, name="offsets")
+        nc.sync.dma_start(offsets[:], offs)
+        table = held.tile([D, S], F32, name="table")
+        nc.sync.dma_start(table[:], x)
+        left_pieces = []
+        for p in range(N // PIECE):
+            left_piece = held.tile([D, PIECE], F32, name=f"left{p}")
+            nc.scalar.dma_start(left_piece[:], left[:, p * PIECE : (p + 1) * PIECE])
+            left_pieces.append(left_piece)
+        layer_weights = held.tile([D, D], BF16, name="layer_weights")
+        nc.sync.dma_start(layer_weights[:], wl)
+        label_weights = held.tile([D, M], BF16, name="label_weights")
+        nc.sync.dma_start(label_weights[:], wp)
+        layer_bias = held.tile([D, 1], F32, name="layer_bias")
+        nc.gpsimd.dma_start(layer_bias[:], bl)
+        label_bias = held.tile([M, 1], F32, name="label_bias")
+        nc.gpsimd.dma_start(label_bias[:], bp)
+
+        layer_bias_twice = held.tile([D, 1], F32, name="layer_bias_twice")
+        nc.gpsimd.tensor_tensor(layer_bias_twice[:], layer_bias[:], layer_bias[:], ADD)
+
+        for p in range(N // PIECE):
+            nodes = slice(p * PIECE, (p + 1) * PIECE)
+            piece_offsets = offsets[:, p * PIECE_OFFSET_COLUMNS : (p + 1) * PIECE_OFFSET_COLUMNS]
+
+            child_sum = work.tile([D, PIECE], F32, name="child_sum")
+            nc.vector.tensor_tensor(child_sum[:], table[:].indirect(piece_offsets), left_pieces[p][:], ADD)
+            child_sum_bf16 = work.tile([D, PIECE], BF16, name="child_sum_bf16")
+            nc.vector.tensor_copy(child_sum_bf16[:], child_sum[:])
+
+            layer_product = psum.tile([D, PIECE], F32, name="layer_product")
+            nc.tensor.matmul(layer_product[:], layer_weights[:], child_sum_bf16[:], start=True, stop=True)
+            state = work.tile([D, PIECE], BF16, name="state")
+            nc.scalar.activation(state[:], layer_product[:], RELU, bias=layer_bias_twice[:])
+
+            label_product = psum.tile([M, PIECE], F32, name="label_product")
+            nc.tensor.matmul(label_product[:], label_weights[:], state[:], start=True, stop=True)
+            scores = work.tile([M, PIECE], F32, name="scores")
+            nc.scalar.activation(scores[:], label_product[:], IDENTITY, bias=label_bias[:])
+            nc.sync.dma_start(out[:, nodes], scores[:])

@@ -32,12 +32,12 @@ def tile_rnn_model_kernel(tc, x, left, wl, bl, wp, bp, offs, out):
             left_pieces.append(left_piece)
         layer_weights = held.tile([D, D], BF16, name="layer_weights")
         nc.sync.dma_start(layer_weights[:], wl)
-        label_weights = held.tile([D, M], BF16, name="label_weights")
-        nc.sync.dma_start(label_weights[:], wp)
         layer_bias = held.tile([D, 1], F32, name="layer_bias")
-        nc.gpsimd.dma_start(layer_bias[:], bl)
+        nc.sync.dma_start(layer_bias[:], bl)
+        label_weights = held.tile([D, M], BF16, name="label_weights")
+        nc.scalar.dma_start(label_weights[:], wp)
         label_bias = held.tile([M, 1], F32, name="label_bias")
-        nc.gpsimd.dma_start(label_bias[:], bp)
+        nc.scalar.dma_start(label_bias[:], bp)
 
         layer_bias_twice = held.tile([D, 1], F32, name="layer_bias_twice")
         nc.gpsimd.tensor_tensor(layer_bias_twice[:], layer_bias[:], layer_bias[:], ADD)

@@ -39,6 +39,11 @@ def tile_rnn_model_kernel(tc, x, left, wl, bl, wp, bp, offs, out):
         label_bias = held.tile([M, 1], F32, name="label_bias")
         nc.scalar.dma_start(label_bias[:], bp)
 
+        scratch = held.tile([D, 1], F32, name="scratch")
+        nc.vector.memset(scratch[:], 0.0)
+        scratch_out = held.tile([D, 1], F32, name="scratch_out")
+        nc.scalar.activation(scratch_out[:], scratch[:], RELU)
+
         layer_bias_twice = held.tile([D, 1], F32, name="layer_bias_twice")
         nc.gpsimd.tensor_tensor(layer_bias_twice[:], layer_bias[:], layer_bias[:], ADD)
 

@@ -5,10 +5,10 @@ BF16 = mybir.dt.bfloat16
 U16 = mybir.dt.uint16
 ADD = mybir.AluOpType.add
 RELU = mybir.ActivationFunctionType.Relu
-IDENTITY = mybir.ActivationFunctionType.Identity
 
 D, S, N, M = 128, 256, 512, 128
-PIECE = 256
+PIECE = 128
+PIECES_IN_HALF = N // 2 // PIECE
 PIECE_OFFSET_COLUMNS = PIECE // 16
 
 FLOPS = 2 * D * D * N + 2 * D * M * N
@@ -18,18 +18,19 @@ def tile_rnn_model_kernel(tc, x, left, wl, bl, wp, bp, offs, out):
     nc = tc.nc
     with (
         tc.tile_pool(name="held", bufs=1) as held,
-        tc.tile_pool(name="work", bufs=2) as work,
-        tc.psum_pool(name="psum", bufs=2) as psum,
+        tc.tile_pool(name="work", bufs=N // PIECE) as work,
+        tc.tile_pool(name="stored", bufs=N // PIECE) as stored,
+        tc.psum_pool(name="psum", bufs=N // PIECE) as psum,
     ):
         offsets = held.tile([D, N // 16], U16, name="offsets")
         nc.sync.dma_start(offsets[:], offs)
         table = held.tile([D, S], F32, name="table")
         nc.sync.dma_start(table[:], x)
-        left_pieces = []
-        for p in range(N // PIECE):
-            left_piece = held.tile([D, PIECE], F32, name=f"left{p}")
-            nc.scalar.dma_start(left_piece[:], left[:, p * PIECE : (p + 1) * PIECE])
-            left_pieces.append(left_piece)
+        left_halves = []
+        for half in range(2):
+            left_half = held.tile([D, N // 2], F32, name=f"left_half{half}")
+            nc.scalar.dma_start(left_half[:], left[:, half * (N // 2) : (half + 1) * (N // 2)])
+            left_halves.append(left_half)
         layer_weights = held.tile([D, D], BF16, name="layer_weights")
         nc.sync.dma_start(layer_weights[:], wl)
         layer_bias = held.tile([D, 1], F32, name="layer_bias")
@@ -49,10 +50,11 @@ def tile_rnn_model_kernel(tc, x, left, wl, bl, wp, bp, offs, out):
 
         for p in range(N // PIECE):
             nodes = slice(p * PIECE, (p + 1) * PIECE)
+            left_piece = left_halves[p // PIECES_IN_HALF][:, (p % PIECES_IN_HALF) * PIECE : (p % PIECES_IN_HALF + 1) * PIECE]
             piece_offsets = offsets[:, p * PIECE_OFFSET_COLUMNS : (p + 1) * PIECE_OFFSET_COLUMNS]
 
             child_sum = work.tile([D, PIECE], F32, name="child_sum")
-            nc.vector.tensor_tensor(child_sum[:], table[:].indirect(piece_offsets), left_pieces[p][:], ADD)
+            nc.vector.tensor_tensor(child_sum[:], table[:].indirect(piece_offsets), left_piece, ADD)
             child_sum_bf16 = work.tile([D, PIECE], BF16, name="child_sum_bf16")
             nc.vector.tensor_copy(child_sum_bf16[:], child_sum[:])
 
@@ -63,6 +65,6 @@ def tile_rnn_model_kernel(tc, x, left, wl, bl, wp, bp, offs, out):
 
             label_product = psum.tile([M, PIECE], F32, name="label_product")
             nc.tensor.matmul(label_product[:], label_weights[:], state[:], start=True, stop=True)
-            scores = work.tile([M, PIECE], F32, name="scores")
-            nc.scalar.activation(scores[:], label_product[:], IDENTITY, bias=label_bias[:])
+            scores = stored.tile([M, PIECE], F32, name="scores")
+            nc.vector.tensor_scalar(scores[:], label_product[:], label_bias[:], None, ADD)
             nc.sync.dma_start(out[:, nodes], scores[:])

@@ -56,7 +56,7 @@ def tile_rnn_model_kernel(tc, x, left, wl, bl, wp, bp, offs, out):
             child_sum = work.tile([D, PIECE], F32, name="child_sum")
             nc.vector.tensor_tensor(child_sum[:], table[:].indirect(piece_offsets), left_piece, ADD)
             child_sum_bf16 = work.tile([D, PIECE], BF16, name="child_sum_bf16")
-            nc.vector.tensor_copy(child_sum_bf16[:], child_sum[:])
+            nc.scalar.copy(child_sum_bf16[:], child_sum[:])
 
             layer_product = psum.tile([D, PIECE], F32, name="layer_product")
             nc.tensor.matmul(layer_product[:], layer_weights[:], child_sum_bf16[:], start=True, stop=True)

@@ -10,6 +10,8 @@ D, S, N, M = 128, 256, 512, 128
 PIECE = 128
 PIECES_IN_HALF = N // 2 // PIECE
 PIECE_OFFSET_COLUMNS = PIECE // 16
+WARM_COLUMNS = 512
+WARM_MATMULS = 5
 
 FLOPS = 2 * D * D * N + 2 * D * M * N
 
@@ -20,7 +22,8 @@ def tile_rnn_model_kernel(tc, x, left, wl, bl, wp, bp, offs, out):
         tc.tile_pool(name="held", bufs=1) as held,
         tc.tile_pool(name="work", bufs=N // PIECE) as work,
         tc.tile_pool(name="stored", bufs=N // PIECE) as stored,
-        tc.psum_pool(name="psum", bufs=N // PIECE) as psum,
+        tc.psum_pool(name="psum", bufs=3) as psum,
+        tc.psum_pool(name="warm_psum", bufs=1) as warm_psum,
     ):
         offsets = held.tile([D, N // 16], U16, name="offsets")
         nc.sync.dma_start(offsets[:], offs)
@@ -44,6 +47,12 @@ def tile_rnn_model_kernel(tc, x, left, wl, bl, wp, bp, offs, out):
         nc.vector.memset(scratch[:], 0.0)
         scratch_out = held.tile([D, 1], F32, name="scratch_out")
         nc.scalar.activation(scratch_out[:], scratch[:], RELU)
+
+        zeros = held.tile([D, WARM_COLUMNS], BF16, name="zeros")
+        nc.vector.memset(zeros[:], 0.0)
+        warm_product = warm_psum.tile([D, WARM_COLUMNS], F32, name="warm_product")
+        for _ in range(WARM_MATMULS):
+            nc.tensor.matmul(warm_product[:], zeros[:, :D], zeros[:], start=True, stop=True)
 
         layer_bias_twice = held.tile([D, 1], F32, name="layer_bias_twice")
         nc.gpsimd.tensor_tensor(layer_bias_twice[:], layer_bias[:], layer_bias[:], ADD)

@@ -7,9 +7,9 @@ ADD = mybir.AluOpType.add
 RELU = mybir.ActivationFunctionType.Relu
 
 D, S, N, M = 128, 256, 512, 128
-PIECE = 128
-PIECES_IN_HALF = N // 2 // PIECE
-PIECE_OFFSET_COLUMNS = PIECE // 16
+PIECE_WIDTHS = (128, 128, 128, 128)
+assert sum(PIECE_WIDTHS) == N
+OFFSETS_IN_COLUMN = 16
 WARM_COLUMNS = 512
 WARM_MATMULS = 5
 
@@ -20,27 +20,25 @@ def tile_rnn_model_kernel(tc, x, left, wl, bl, wp, bp, offs, out):
     nc = tc.nc
     with (
         tc.tile_pool(name="held", bufs=1) as held,
-        tc.tile_pool(name="work", bufs=N // PIECE) as work,
-        tc.tile_pool(name="stored", bufs=N // PIECE) as stored,
+        tc.tile_pool(name="work", bufs=len(PIECE_WIDTHS)) as work,
+        tc.tile_pool(name="stored", bufs=len(PIECE_WIDTHS)) as stored,
         tc.psum_pool(name="psum", bufs=3) as psum,
         tc.psum_pool(name="warm_psum", bufs=1) as warm_psum,
     ):
-        offsets = held.tile([D, N // 16], U16, name="offsets")
-        nc.sync.dma_start(offsets[:], offs)
+        offsets = held.tile([D, N // OFFSETS_IN_COLUMN], U16, name="offsets")
         table = held.tile([D, S], F32, name="table")
-        nc.sync.dma_start(table[:], x)
-        left_halves = []
-        for half in range(2):
-            left_half = held.tile([D, N // 2], F32, name=f"left_half{half}")
-            nc.scalar.dma_start(left_half[:], left[:, half * (N // 2) : (half + 1) * (N // 2)])
-            left_halves.append(left_half)
+        left_states = held.tile([D, N], F32, name="left_states")
         layer_weights = held.tile([D, D], BF16, name="layer_weights")
-        nc.sync.dma_start(layer_weights[:], wl)
         layer_bias = held.tile([D, 1], F32, name="layer_bias")
-        nc.sync.dma_start(layer_bias[:], bl)
         label_weights = held.tile([D, M], BF16, name="label_weights")
-        nc.scalar.dma_start(label_weights[:], wp)
         label_bias = held.tile([M, 1], F32, name="label_bias")
+        nc.sync.dma_start(offsets[:], offs)
+        nc.sync.dma_start(table[:], x)
+        nc.scalar.dma_start(left_states[:, : N // 2], left[:, : N // 2])
+        nc.scalar.dma_start(left_states[:, N // 2 :], left[:, N // 2 :])
+        nc.sync.dma_start(layer_weights[:], wl)
+        nc.sync.dma_start(layer_bias[:], bl)
+        nc.scalar.dma_start(label_weights[:], wp)
         nc.scalar.dma_start(label_bias[:], bp)
 
         scratch = held.tile([D, 1], F32, name="scratch")
@@ -57,23 +55,27 @@ def tile_rnn_model_kernel(tc, x, left, wl, bl, wp, bp, offs, out):
         layer_bias_twice = held.tile([D, 1], F32, name="layer_bias_twice")
         nc.gpsimd.tensor_tensor(layer_bias_twice[:], layer_bias[:], layer_bias[:], ADD)
 
-        for p in range(N // PIECE):
-            nodes = slice(p * PIECE, (p + 1) * PIECE)
-            left_piece = left_halves[p // PIECES_IN_HALF][:, (p % PIECES_IN_HALF) * PIECE : (p % PIECES_IN_HALF + 1) * PIECE]
-            piece_offsets = offsets[:, p * PIECE_OFFSET_COLUMNS : (p + 1) * PIECE_OFFSET_COLUMNS]
+        first = 0
+        for width in PIECE_WIDTHS:
+            nodes = slice(first, first + width)
+            piece_offsets = offsets[:, first // OFFSETS_IN_COLUMN : (first + width) // OFFSETS_IN_COLUMN]
+            first += width
 
-            child_sum = work.tile([D, PIECE], F32, name="child_sum")
-            nc.vector.tensor_tensor(child_sum[:], table[:].indirect(piece_offsets), left_piece, ADD)
-            child_sum_bf16 = work.tile([D, PIECE], BF16, name="child_sum_bf16")
-            nc.scalar.copy(child_sum_bf16[:], child_sum[:])
+            child_sum = work.tile([D, width], F32, name="child_sum")
+            nc.vector.tensor_tensor(child_sum[:], table[:].indirect(piece_offsets), left_states[:, nodes], ADD)
+            child_sum_bf16 = work.tile([D, width], BF16, name="child_sum_bf16")
+            if first < N:
+                nc.scalar.copy(child_sum_bf16[:], child_sum[:])
+            else:
+                nc.vector.tensor_copy(child_sum_bf16[:], child_sum[:])
 
-            layer_product = psum.tile([D, PIECE], F32, name="layer_product")
+            layer_product = psum.tile([D, width], F32, name="layer_product")
             nc.tensor.matmul(layer_product[:], layer_weights[:], child_sum_bf16[:], start=True, stop=True)
-            state = work.tile([D, PIECE], BF16, name="state")
+            state = work.tile([D, width], BF16, name="state")
             nc.scalar.activation(state[:], layer_product[:], RELU, bias=layer_bias_twice[:])
 
-            label_product = psum.tile([M, PIECE], F32, name="label_product")
+            label_product = psum.tile([M, width], F32, name="label_product")
             nc.tensor.matmul(label_product[:], label_weights[:], state[:], start=True, stop=True)
-            scores = stored.tile([M, PIECE], F32, name="scores")
+            scores = stored.tile([M, width], F32, name="scores")
             nc.vector.tensor_scalar(scores[:], label_product[:], label_bias[:], None, ADD)
             nc.sync.dma_start(out[:, nodes], scores[:])

@@ -22,8 +22,7 @@ def tile_rnn_model_kernel(tc, x, left, wl, bl, wp, bp, offs, out):
         tc.tile_pool(name="held", bufs=1) as held,
         tc.tile_pool(name="work", bufs=len(PIECE_WIDTHS)) as work,
         tc.tile_pool(name="stored", bufs=len(PIECE_WIDTHS)) as stored,
-        tc.psum_pool(name="psum", bufs=3) as psum,
-        tc.psum_pool(name="warm_psum", bufs=1) as warm_psum,
+        tc.psum_pool(name="psum", bufs=len(PIECE_WIDTHS)) as psum,
     ):
         offsets = held.tile([D, N // OFFSETS_IN_COLUMN], U16, name="offsets")
         table = held.tile([D, S], F32, name="table")
@@ -48,7 +47,7 @@ def tile_rnn_model_kernel(tc, x, left, wl, bl, wp, bp, offs, out):
 
         zeros = held.tile([D, WARM_COLUMNS], BF16, name="zeros")
         nc.vector.memset(zeros[:], 0.0)
-        warm_product = warm_psum.tile([D, WARM_COLUMNS], F32, name="warm_product")
+        warm_product = psum.tile([D, WARM_COLUMNS], F32, name="warm_product", tag="label_product")
         for _ in range(WARM_MATMULS):
             nc.tensor.matmul(warm_product[:], zeros[:, :D], zeros[:], start=True, stop=True)
 

@@ -31,8 +31,8 @@ def tile_rnn_model_kernel(tc, x, left, wl, bl, wp, bp, offs, out):
         layer_bias = held.tile([D, 1], F32, name="layer_bias")
         label_weights = held.tile([D, M], BF16, name="label_weights")
         label_bias = held.tile([M, 1], F32, name="label_bias")
-        nc.sync.dma_start(offsets[:], offs)
         nc.sync.dma_start(table[:], x)
+        nc.sync.dma_start(offsets[:], offs)
         nc.scalar.dma_start(left_states[:, : N // 2], left[:, : N // 2])
         nc.scalar.dma_start(left_states[:, N // 2 :], left[:, N // 2 :])
         nc.sync.dma_start(layer_weights[:], wl)

@@ -4,6 +4,7 @@ F32 = mybir.dt.float32
 BF16 = mybir.dt.bfloat16
 U16 = mybir.dt.uint16
 ADD = mybir.AluOpType.add
+MULT = mybir.AluOpType.mult
 RELU = mybir.ActivationFunctionType.Relu
 
 D, S, N, M = 128, 256, 512, 128
@@ -51,9 +52,6 @@ def tile_rnn_model_kernel(tc, x, left, wl, bl, wp, bp, offs, out):
         for _ in range(WARM_MATMULS):
             nc.tensor.matmul(warm_product[:], zeros[:, :D], zeros[:], start=True, stop=True)
 
-        layer_bias_twice = held.tile([D, 1], F32, name="layer_bias_twice")
-        nc.gpsimd.tensor_tensor(layer_bias_twice[:], layer_bias[:], layer_bias[:], ADD)
-
         first = 0
         for width in PIECE_WIDTHS:
             nodes = slice(first, first + width)
@@ -70,11 +68,11 @@ def tile_rnn_model_kernel(tc, x, left, wl, bl, wp, bp, offs, out):
 
             layer_product = psum.tile([D, width], F32, name="layer_product")
             nc.tensor.matmul(layer_product[:], layer_weights[:], child_sum_bf16[:], start=True, stop=True)
-            state = work.tile([D, width], BF16, name="state")
-            nc.scalar.activation(state[:], layer_product[:], RELU, bias=layer_bias_twice[:])
+            half_state = work.tile([D, width], BF16, name="half_state")
+            nc.scalar.activation(half_state[:], layer_product[:], RELU, bias=layer_bias[:], scale=0.5)
 
             label_product = psum.tile([M, width], F32, name="label_product")
-            nc.tensor.matmul(label_product[:], label_weights[:], state[:], start=True, stop=True)
+            nc.tensor.matmul(label_product[:], label_weights[:], half_state[:], start=True, stop=True)
             scores = stored.tile([M, width], F32, name="scores")
-            nc.vector.tensor_scalar(scores[:], label_product[:], label_bias[:], None, ADD)
+            nc.vector.tensor_scalar(scores[:], label_product[:], 2.0, label_bias[:], MULT, ADD)
             nc.sync.dma_start(out[:, nodes], scores[:])

import concourse.mybir as mybir

F32 = mybir.dt.float32
BF16 = mybir.dt.bfloat16
U16 = mybir.dt.uint16
ADD = mybir.AluOpType.add
MULT = mybir.AluOpType.mult
RELU = mybir.ActivationFunctionType.Relu

D, S, N, M = 128, 256, 512, 128
PIECE_WIDTHS = (128, 128, 128, 128)
assert sum(PIECE_WIDTHS) == N
OFFSETS_IN_COLUMN = 16
WARM_COLUMNS = 512
WARM_MATMULS = 5

FLOPS = 2 * D * D * N + 2 * D * M * N


def tile_rnn_model_kernel(tc, x, left, wl, bl, wp, bp, offs, out):
    nc = tc.nc
    with (
        tc.tile_pool(name="held", bufs=1) as held,
        tc.tile_pool(name="work", bufs=len(PIECE_WIDTHS)) as work,
        tc.tile_pool(name="stored", bufs=len(PIECE_WIDTHS)) as stored,
        tc.psum_pool(name="psum", bufs=len(PIECE_WIDTHS)) as psum,
    ):
        offsets = held.tile([D, N // OFFSETS_IN_COLUMN], U16, name="offsets")
        table = held.tile([D, S], F32, name="table")
        left_states = held.tile([D, N], F32, name="left_states")
        layer_weights = held.tile([D, D], BF16, name="layer_weights")
        layer_bias = held.tile([D, 1], F32, name="layer_bias")
        label_weights = held.tile([D, M], BF16, name="label_weights")
        label_bias = held.tile([M, 1], F32, name="label_bias")
        nc.sync.dma_start(table[:], x)
        nc.sync.dma_start(offsets[:], offs)
        nc.scalar.dma_start(left_states[:, : N // 2], left[:, : N // 2])
        nc.scalar.dma_start(left_states[:, N // 2 :], left[:, N // 2 :])
        nc.sync.dma_start(layer_weights[:], wl)
        nc.sync.dma_start(layer_bias[:], bl)
        nc.scalar.dma_start(label_weights[:], wp)
        nc.scalar.dma_start(label_bias[:], bp)

        scratch = held.tile([D, 1], F32, name="scratch")
        nc.vector.memset(scratch[:], 0.0)
        scratch_out = held.tile([D, 1], F32, name="scratch_out")
        nc.scalar.activation(scratch_out[:], scratch[:], RELU)

        zeros = held.tile([D, WARM_COLUMNS], BF16, name="zeros")
        nc.vector.memset(zeros[:], 0.0)
        warm_product = psum.tile([D, WARM_COLUMNS], F32, name="warm_product", tag="label_product")
        for _ in range(WARM_MATMULS):
            nc.tensor.matmul(warm_product[:], zeros[:, :D], zeros[:], start=True, stop=True)

        first = 0
        for width in PIECE_WIDTHS:
            nodes = slice(first, first + width)
            piece_offsets = offsets[:, first // OFFSETS_IN_COLUMN : (first + width) // OFFSETS_IN_COLUMN]
            first += width

            child_sum = work.tile([D, width], F32, name="child_sum")
            nc.vector.tensor_tensor(child_sum[:], table[:].indirect(piece_offsets), left_states[:, nodes], ADD)
            child_sum_bf16 = work.tile([D, width], BF16, name="child_sum_bf16")
            if first < N:
                nc.scalar.copy(child_sum_bf16[:], child_sum[:])
            else:
                nc.vector.tensor_copy(child_sum_bf16[:], child_sum[:])

            layer_product = psum.tile([D, width], F32, name="layer_product")
            nc.tensor.matmul(layer_product[:], layer_weights[:], child_sum_bf16[:], start=True, stop=True)
            half_state = work.tile([D, width], BF16, name="half_state")
            nc.scalar.activation(half_state[:], layer_product[:], RELU, bias=layer_bias[:], scale=0.5)

            label_product = psum.tile([M, width], F32, name="label_product")
            nc.tensor.matmul(label_product[:], label_weights[:], half_state[:], start=True, stop=True)
            scores = stored.tile([M, width], F32, name="scores")
            nc.vector.tensor_scalar(scores[:], label_product[:], 2.0, label_bias[:], MULT, ADD)
            nc.sync.dma_start(out[:, nodes], scores[:])
